import numpy as np
import ml_dtypes


def mxq(x, axis, fmt="e4m3"):
    dtype, down = {"e4m3": (ml_dtypes.float8_e4m3fn, 7), "e5m2": (ml_dtypes.float8_e5m2, 14)}[fmt]
    v = np.moveaxis(np.asarray(x, np.float32).astype(ml_dtypes.bfloat16).astype(np.float64), axis, -1)
    blocks = v.reshape(v.shape[:-1] + (-1, 32))
    amax = np.abs(blocks).max(-1, keepdims=True)
    byte = np.maximum(np.where(amax > 0, np.frexp(amax)[1] - 1 + 127, 0) - down, 1)
    scale = np.exp2(byte - 127.0)
    codes = (blocks / scale).astype(np.float32).astype(dtype).astype(np.float64)
    return np.moveaxis((codes * scale).reshape(v.shape), -1, axis)


WIDE = False


def mx_kscale(k):
    if not WIDE:
        return np.ones(k)
    levels = np.array([20, -20, 10, -10, 0])
    a = np.random.permutation(np.resize(levels, k // 512 * 4)).reshape(k // 512, 4)
    idx = np.arange(k)
    return np.exp2(a[idx // 512, idx % 128 // 32])


BF16 = ml_dtypes.bfloat16


def bf(x):
    return np.asarray(x, np.float32).astype(BF16)


def f64(x):
    return np.asarray(x).astype(np.float64)


B, N, F, T, DE, FO, K = 2, 1024, 16, 32, 16, 32, 3
C = F * T


def setup_inputs():
    s = mx_kscale(N)
    supports = np.abs(np.random.standard_normal((N, N))) * 0.4 / np.sqrt(N)
    cheb_2 = np.random.standard_normal((N, N)) * 0.8 / np.sqrt(N)
    spatial_attention = np.random.random((B, N, N)) * s[None, None, :]
    x = np.random.standard_normal((B, N, F, T))
    g = np.random.standard_normal((K, B, N, F, T)) * np.exp2(np.random.randint(-12, 1, (K, B, N, 1, 1))) * 8.0
    g = g / s[None, None, :, None, None]
    return {"supports": bf(supports), "cheb_2": bf(cheb_2), "spatial_attention": bf(spatial_attention),
            "x": bf(x), "grad_out": bf(g)}


def reference(supports, cheb_2, spatial_attention, x, grad_out):
    at = f64(spatial_attention)
    g = f64(grad_out).reshape(K, B, N, C)
    r0 = np.diagonal(at, axis1=1, axis2=2)[:, :, None] * g[0]
    r1 = mxq(f64(supports)[None] * at, 2, "e4m3") @ mxq(g[1], 1, "e5m2")
    r2 = mxq(f64(cheb_2)[None] * at, 2, "e4m3") @ mxq(g[2], 1, "e5m2")
    return (r0 + r1 + r2).reshape(B, N, F, T)

@@ -1,0 +1,212 @@
+from contextlib import ExitStack
+
+import concourse.mybir as mybir
+from concourse.masks import make_identity
+
+BF16 = mybir.dt.bfloat16
+F32 = mybir.dt.float32
+U32 = mybir.dt.uint32
+U8 = mybir.dt.uint8
+E4M3_X4 = mybir.dt.float8_e4m3fn_x4
+E5M2_X4 = mybir.dt.float8_e5m2_x4
+MULT = mybir.AluOpType.mult
+ADD = mybir.AluOpType.add
+
+P = 128
+SAMPLES = 2
+NODES = 1024
+CHANNELS = 512
+ORDERS = 2
+PACK = 4
+PASSES = NODES // (P * PACK)
+ROW_TILES = NODES // P
+CHUNK = 2
+CHUNKS = ROW_TILES // CHUNK
+UNITS = SAMPLES * ROW_TILES
+WORDS = P
+FLIPS = NODES // (2 * WORDS)
+
+VECTOR_COLUMNS = (256, 128)
+
+FLOPS = 2 * SAMPLES * ORDERS * NODES * NODES * CHANNELS
+BYTES = 2 * (2 * NODES * NODES + SAMPLES * NODES * NODES + 3 * SAMPLES * NODES * CHANNELS) + 4 * SAMPLES * NODES * CHANNELS
+
+
+def tile_napl_conv_withsat_pb_kernel(tc, supports, cheb_2, spatial_attention, x, grad_out, out):
+    nc = tc.nc
+
+    matrix_rows = "(p i) m -> p i m"
+    supports_v = supports.rearrange(matrix_rows, i=ROW_TILES)
+    cheb_2_v = cheb_2.rearrange(matrix_rows, i=ROW_TILES)
+    attention_v = spatial_attention.rearrange("b (p i) m -> b p i m", i=ROW_TILES)
+    grad_v = grad_out.rearrange("k b m f t -> k b m (f t)")
+    out_v = out.rearrange("b (p i) f t -> b p i (f t)", i=ROW_TILES)
+    diagonal_v = spatial_attention.rearrange("b n m -> b (n m)")[:, 0 : NODES * NODES : NODES + 1]
+
+    with ExitStack() as stack:
+        stack.enter_context(tc.manual_schedule())
+        keep = stack.enter_context(tc.tile_pool(name="keep", bufs=1))
+        stage = stack.enter_context(tc.tile_pool(name="stage", bufs=3))
+        results = stack.enter_context(tc.tile_pool(name="results", bufs=10))
+        flipped = stack.enter_context(tc.psum_pool(name="flipped", bufs=6))
+        sums = stack.enter_context(tc.psum_pool(name="sums", bufs=2))
+
+        def load_grad_piece(b, o, g):
+            raw = keep.tile([P, PACK, CHANNELS], BF16, name="grad_raw_%d_%d_%d" % (b, o, g))
+            rows = grad_v[o + 1, b].rearrange("(g u p e) c -> g p u (e c)", g=PASSES, u=2, e=2)
+            nc.sync.dma_start(out=raw[:].rearrange("p (u e) c -> p u (e c)", u=2), in_=rows[g])
+            return raw
+
+        def load_chunk(view, c, width, name):
+            raw = keep.tile([P, CHUNK, width], BF16, name="%s_%d" % (name, c))
+            nc.sync.dma_start(out=raw[:], in_=view[:, c * CHUNK : (c + 1) * CHUNK, :])
+            return raw
+
+        pieces = [(o, g) for o in range(ORDERS) for g in range(PASSES)]
+        grad_raw = {}
+        supports_raw, cheb_2_raw = [], []
+        attention_raw = [[], []]
+        grad_0_raw = [[], []]
+        for o, g in pieces:
+            grad_raw[(0, o, g)] = load_grad_piece(0, o, g)
+        diagonal_bf16 = [keep.tile([P, ROW_TILES], BF16, name="diagonal_bf16_%d" % b) for b in range(SAMPLES)]
+        for c in range(CHUNKS):
+            supports_raw.append(load_chunk(supports_v, c, NODES, "supports_raw"))
+            cheb_2_raw.append(load_chunk(cheb_2_v, c, NODES, "cheb_2_raw"))
+            attention_raw[0].append(load_chunk(attention_v[0], c, NODES, "attention_raw_0"))
+            grad_0_raw[0].append(load_chunk(grad_v[0, 0].rearrange("(p i) c -> p i c", i=ROW_TILES), c, CHANNELS, "grad_0_raw_0"))
+            if c == 0:
+                with nc.allow_non_contiguous_dma(reason="2,048 diagonal elements, one to a row of the attention"):
+                    for b in range(SAMPLES):
+                        nc.sync.dma_start(out=diagonal_bf16[b][:], in_=diagonal_v[b].rearrange("(p i) -> p i", i=ROW_TILES))
+            o, g = pieces[c]
+            grad_raw[(1, o, g)] = load_grad_piece(1, o, g)
+        for c in range(CHUNKS):
+            attention_raw[1].append(load_chunk(attention_v[1], c, NODES, "attention_raw_1"))
+            grad_0_raw[1].append(load_chunk(grad_v[0, 1].rearrange("(p i) c -> p i c", i=ROW_TILES), c, CHANNELS, "grad_0_raw_1"))
+
+        identity = keep.tile([P, P], F32)
+        make_identity(nc, identity[:])
+        diagonal = keep.tile([P, SAMPLES, ROW_TILES], F32)
+        for b in range(SAMPLES):
+            nc.gpsimd.tensor_copy(out=diagonal[:, b, :], in_=diagonal_bf16[b][:])
+
+        grad_grouped, grad_codes, grad_scales = {}, {}, {}
+
+        def regroup_grad_piece(b, o, g):
+            raw = grad_raw[(b, o, g)]
+            grouped = stage.tile([P, CHANNELS, PACK], BF16, name="grad_grouped", align_bytes=64)
+            split = VECTOR_COLUMNS[b]
+            nc.vector.tensor_copy(
+                out=grouped[:, :split, :].rearrange("p (c i) t -> p c t i", i=4),
+                in_=raw[:, :, :split].rearrange("p t (c i) -> p c t i", i=4),
+            )
+            nc.scalar.copy(
+                out=grouped[:, split:, :].rearrange("p (c i) t -> p c t i", i=4),
+                in_=raw[:, :, split:].rearrange("p t (c i) -> p c t i", i=4),
+            )
+            grad_grouped[(b, o, g)] = grouped
+
+        def quantise_grad_piece(b, o, g):
+            codes = keep.tile([P, CHANNELS], U32, name="grad_codes_%d_%d_%d" % (b, o, g), align_bytes=64)
+            scales = keep.tile([P, CHANNELS], U8, name="grad_scales_%d_%d_%d" % (b, o, g), align_bytes=64)
+            nc.vector.quantize_mx(
+                out=codes[:].bitcast(E5M2_X4),
+                scales=scales[:],
+                in_=grad_grouped[(b, o, g)][:].rearrange("p c t -> p (c t)"),
+            )
+            grad_codes[(b, o, g)] = codes
+            grad_scales[(b, o, g)] = scales
+
+        weights_t = {}
+        attention_t, products, product_codes, product_scales, unit_sums = {}, {}, {}, {}, {}
+
+        def flip_rows(rows, grouped):
+            words = rows.bitcast(F32)
+            bank = flipped.tile([P, FLIPS, P], F32, name="bank")
+            for j in range(FLIPS):
+                nc.tensor.transpose(bank[:, j, :], words[:, j * WORDS : (j + 1) * WORDS], identity[:])
+            nc.scalar.copy(
+                out=grouped.bitcast(F32).rearrange("p (g n u) -> p g n u", g=PASSES, u=2),
+                in_=bank[:].rearrange("p (g u) n -> p g n u", u=2),
+            )
+
+        def flip(unit):
+            b, i = divmod(unit, ROW_TILES)
+            c, r = divmod(i, CHUNK)
+            if b == 0:
+                weights_t[i] = keep.tile([P, ORDERS * NODES], BF16, name="weights_t_%d" % i)
+                flip_rows(supports_raw[c][:, r, :], weights_t[i][:, :NODES])
+                flip_rows(cheb_2_raw[c][:, r, :], weights_t[i][:, NODES:])
+            attention_t[unit] = stage.tile([P, NODES], BF16, name="attention_t")
+            flip_rows(attention_raw[b][c][:, r, :], attention_t[unit][:])
+
+        def multiply(unit):
+            i = unit % ROW_TILES
+            products[unit] = stage.tile([P, ORDERS * NODES], BF16, name="products", align_bytes=64)
+            nc.vector.tensor_tensor(
+                out=products[unit][:].rearrange("p (o k) -> p o k", o=ORDERS),
+                in0=weights_t[i][:].rearrange("p (o k) -> p o k", o=ORDERS),
+                in1=attention_t[unit][:].unsqueeze(1).to_broadcast([P, ORDERS, NODES]),
+                op=MULT,
+            )
+
+        def quantise(unit):
+            product_codes[unit] = stage.tile([P, ORDERS * PASSES * P], U32, name="product_codes", align_bytes=64)
+            product_scales[unit] = stage.tile([P, ORDERS * PASSES * P], U8, name="product_scales", align_bytes=64)
+            nc.vector.quantize_mx(
+                out=product_codes[unit][:].bitcast(E4M3_X4),
+                scales=product_scales[unit][:],
+                in_=products[unit][:],
+            )
+
+        def contract(unit):
+            b = unit // ROW_TILES
+            unit_sums[unit] = sums.tile([P, CHANNELS], F32, name="unit_sums")
+            for index, (o, g) in enumerate(pieces):
+                n_cols = slice(index * P, (index + 1) * P)
+                nc.tensor.matmul_mx(
+                    out=unit_sums[unit][:],
+                    lhsT=product_codes[unit][:, n_cols].bitcast(E4M3_X4),
+                    lhsT_scale=product_scales[unit][:, n_cols],
+                    rhs=grad_codes[(b, o, g)][:].bitcast(E5M2_X4),
+                    rhs_scale=grad_scales[(b, o, g)][:],
+                    start=(index == 0),
+                    stop=(index == len(pieces) - 1),
+                )
+
+        def finish(unit):
+            b, i = divmod(unit, ROW_TILES)
+            c, r = divmod(i, CHUNK)
+            result = results.tile([P, CHANNELS], F32, name="result")
+            nc.vector.scalar_tensor_tensor(
+                out=result[:],
+                in0=grad_0_raw[b][c][:, r, :],
+                scalar=diagonal[:, b, i : i + 1],
+                in1=unit_sums[unit][:],
+                op0=MULT,
+                op1=ADD,
+            )
+            nc.sync.dma_start(out=out_v[b][:, i, :], in_=result[:])
+
+        for index, (o, g) in enumerate(pieces):
+            regroup_grad_piece(0, o, g)
+            if index > 0:
+                quantise_grad_piece(0, *pieces[index - 1])
+        flip(0)
+        quantise_grad_piece(0, *pieces[-1])
+
+        for s in range(UNITS + 2):
+            if s + 1 < UNITS:
+                flip(s + 1)
+            if 1 <= s <= UNITS:
+                quantise(s - 1)
+                contract(s - 1)
+            if s < UNITS:
+                multiply(s)
+            if s >= 2:
+                finish(s - 2)
+            if s < ROW_TILES and s % CHUNK == 0:
+                regroup_grad_piece(1, *pieces[s // CHUNK])
+            if s < ROW_TILES and s % CHUNK == 1:
+                quantise_grad_piece(1, *pieces[s // CHUNK])

@@ -20,13 +20,11 @@ ORDERS = 2
 PACK = 4
 PASSES = NODES // (P * PACK)
 ROW_TILES = NODES // P
-CHUNK = 2
-CHUNKS = ROW_TILES // CHUNK
-UNITS = SAMPLES * ROW_TILES
-WORDS = P
-FLIPS = NODES // (2 * WORDS)
+FLIPS = NODES // (2 * P)
 
-VECTOR_COLUMNS = (256, 128)
+TILES_BEFORE_GRAD = 2
+FINISH_LAG = 2
+VECTOR_COLUMNS = 256
 
 FLOPS = 2 * SAMPLES * ORDERS * NODES * NODES * CHANNELS
 BYTES = 2 * (2 * NODES * NODES + SAMPLES * NODES * NODES + 3 * SAMPLES * NODES * CHANNELS) + 4 * SAMPLES * NODES * CHANNELS
@@ -35,55 +33,59 @@ BYTES = 2 * (2 * NODES * NODES + SAMPLES * NODES * NODES + 3 * SAMPLES * NODES *
 def tile_napl_conv_withsat_pb_kernel(tc, supports, cheb_2, spatial_attention, x, grad_out, out):
     nc = tc.nc
 
-    matrix_rows = "(p i) m -> p i m"
-    supports_v = supports.rearrange(matrix_rows, i=ROW_TILES)
-    cheb_2_v = cheb_2.rearrange(matrix_rows, i=ROW_TILES)
-    attention_v = spatial_attention.rearrange("b (p i) m -> b p i m", i=ROW_TILES)
+    supports_v = supports.rearrange("(i p) m -> i p m", p=P)
+    cheb_2_v = cheb_2.rearrange("(i p) m -> i p m", p=P)
+    attention_v = spatial_attention.rearrange("b (i p) m -> b i p m", p=P)
     grad_v = grad_out.rearrange("k b m f t -> k b m (f t)")
-    out_v = out.rearrange("b (p i) f t -> b p i (f t)", i=ROW_TILES)
+    grad_0_v = grad_v[0].rearrange("b (i p) c -> i p b c", p=P)
+    out_v = out.rearrange("b (i p) f t -> b i p (f t)", p=P)
     diagonal_v = spatial_attention.rearrange("b n m -> b (n m)")[:, 0 : NODES * NODES : NODES + 1]
 
     with ExitStack() as stack:
         stack.enter_context(tc.manual_schedule())
         keep = stack.enter_context(tc.tile_pool(name="keep", bufs=1))
-        stage = stack.enter_context(tc.tile_pool(name="stage", bufs=3))
+        stage = stack.enter_context(tc.tile_pool(name="stage", bufs=2))
         results = stack.enter_context(tc.tile_pool(name="results", bufs=10))
-        flipped = stack.enter_context(tc.psum_pool(name="flipped", bufs=6))
-        sums = stack.enter_context(tc.psum_pool(name="sums", bufs=2))
+        flipped = stack.enter_context(tc.psum_pool(name="flipped", bufs=4))
+        sums = stack.enter_context(tc.psum_pool(name="sums", bufs=4))
+
+        pieces = [(b, o, g) for b in range(SAMPLES) for o in range(ORDERS) for g in range(PASSES)]
+        supports_raw, cheb_2_raw, attention_raw, grad_0_raw, grad_raw = {}, {}, {}, {}, {}
+
+        def load_rows(view, name):
+            raw = keep.tile([P, NODES], BF16, name=name)
+            nc.sync.dma_start(out=raw[:], in_=view)
+            return raw
+
+        def load_matrices(i):
+            supports_raw[i] = load_rows(supports_v[i], "supports_raw_%d" % i)
+            cheb_2_raw[i] = load_rows(cheb_2_v[i], "cheb_2_raw_%d" % i)
+            for b in range(SAMPLES):
+                attention_raw[(b, i)] = load_rows(attention_v[b, i], "attention_raw_%d_%d" % (b, i))
+
+        def load_grad_0(i):
+            grad_0_raw[i] = keep.tile([P, SAMPLES, CHANNELS], BF16, name="grad_0_raw_%d" % i)
+            nc.sync.dma_start(out=grad_0_raw[i][:], in_=grad_0_v[i])
 
         def load_grad_piece(b, o, g):
             raw = keep.tile([P, PACK, CHANNELS], BF16, name="grad_raw_%d_%d_%d" % (b, o, g))
             rows = grad_v[o + 1, b].rearrange("(g u p e) c -> g p u (e c)", g=PASSES, u=2, e=2)
             nc.sync.dma_start(out=raw[:].rearrange("p (u e) c -> p u (e c)", u=2), in_=rows[g])
-            return raw
+            grad_raw[(b, o, g)] = raw
 
-        def load_chunk(view, c, width, name):
-            raw = keep.tile([P, CHUNK, width], BF16, name="%s_%d" % (name, c))
-            nc.sync.dma_start(out=raw[:], in_=view[:, c * CHUNK : (c + 1) * CHUNK, :])
-            return raw
-
-        pieces = [(o, g) for o in range(ORDERS) for g in range(PASSES)]
-        grad_raw = {}
-        supports_raw, cheb_2_raw = [], []
-        attention_raw = [[], []]
-        grad_0_raw = [[], []]
-        for o, g in pieces:
-            grad_raw[(0, o, g)] = load_grad_piece(0, o, g)
         diagonal_bf16 = [keep.tile([P, ROW_TILES], BF16, name="diagonal_bf16_%d" % b) for b in range(SAMPLES)]
-        for c in range(CHUNKS):
-            supports_raw.append(load_chunk(supports_v, c, NODES, "supports_raw"))
-            cheb_2_raw.append(load_chunk(cheb_2_v, c, NODES, "cheb_2_raw"))
-            attention_raw[0].append(load_chunk(attention_v[0], c, NODES, "attention_raw_0"))
-            grad_0_raw[0].append(load_chunk(grad_v[0, 0].rearrange("(p i) c -> p i c", i=ROW_TILES), c, CHANNELS, "grad_0_raw_0"))
-            if c == 0:
-                with nc.allow_non_contiguous_dma(reason="2,048 diagonal elements, one to a row of the attention"):
-                    for b in range(SAMPLES):
-                        nc.sync.dma_start(out=diagonal_bf16[b][:], in_=diagonal_v[b].rearrange("(p i) -> p i", i=ROW_TILES))
-            o, g = pieces[c]
-            grad_raw[(1, o, g)] = load_grad_piece(1, o, g)
-        for c in range(CHUNKS):
-            attention_raw[1].append(load_chunk(attention_v[1], c, NODES, "attention_raw_1"))
-            grad_0_raw[1].append(load_chunk(grad_v[0, 1].rearrange("(p i) c -> p i c", i=ROW_TILES), c, CHANNELS, "grad_0_raw_1"))
+
+        for i in range(TILES_BEFORE_GRAD):
+            load_matrices(i)
+        for piece in pieces:
+            load_grad_piece(*piece)
+        with nc.allow_non_contiguous_dma(reason="2,048 diagonal elements, one to a row of the attention"):
+            for b in range(SAMPLES):
+                nc.sync.dma_start(out=diagonal_bf16[b][:], in_=diagonal_v[b].rearrange("(i p) -> p i", p=P))
+        for i in range(TILES_BEFORE_GRAD, ROW_TILES + FINISH_LAG):
+            if i < ROW_TILES:
+                load_matrices(i)
+            load_grad_0(i - FINISH_LAG)
 
         identity = keep.tile([P, P], F32)
         make_identity(nc, identity[:])
@@ -93,120 +95,114 @@ def tile_napl_conv_withsat_pb_kernel(tc, supports, cheb_2, spatial_attention, x,
 
         grad_grouped, grad_codes, grad_scales = {}, {}, {}
 
-        def regroup_grad_piece(b, o, g):
-            raw = grad_raw[(b, o, g)]
-            grouped = stage.tile([P, CHANNELS, PACK], BF16, name="grad_grouped", align_bytes=64)
-            split = VECTOR_COLUMNS[b]
+        def regroup_grad_piece(piece):
+            raw = grad_raw[piece]
+            grouped = stage.tile([P, CHANNELS, PACK], BF16, name="grad_grouped", bufs=3, align_bytes=64)
             nc.vector.tensor_copy(
-                out=grouped[:, :split, :].rearrange("p (c i) t -> p c t i", i=4),
-                in_=raw[:, :, :split].rearrange("p t (c i) -> p c t i", i=4),
+                out=grouped[:, :VECTOR_COLUMNS, :].rearrange("p (c i) t -> p c t i", i=4),
+                in_=raw[:, :, :VECTOR_COLUMNS].rearrange("p t (c i) -> p c t i", i=4),
             )
             nc.scalar.copy(
-                out=grouped[:, split:, :].rearrange("p (c i) t -> p c t i", i=4),
-                in_=raw[:, :, split:].rearrange("p t (c i) -> p c t i", i=4),
+                out=grouped[:, VECTOR_COLUMNS:, :].rearrange("p (c i) t -> p c t i", i=4),
+                in_=raw[:, :, VECTOR_COLUMNS:].rearrange("p t (c i) -> p c t i", i=4),
             )
-            grad_grouped[(b, o, g)] = grouped
+            grad_grouped[piece] = grouped
 
-        def quantise_grad_piece(b, o, g):
-            codes = keep.tile([P, CHANNELS], U32, name="grad_codes_%d_%d_%d" % (b, o, g), align_bytes=64)
-            scales = keep.tile([P, CHANNELS], U8, name="grad_scales_%d_%d_%d" % (b, o, g), align_bytes=64)
+        def quantise_grad_piece(piece):
+            codes = keep.tile([P, CHANNELS], U32, name="grad_codes_%d_%d_%d" % piece, align_bytes=64)
+            scales = keep.tile([P, CHANNELS], U8, name="grad_scales_%d_%d_%d" % piece, align_bytes=64)
             nc.vector.quantize_mx(
                 out=codes[:].bitcast(E5M2_X4),
                 scales=scales[:],
-                in_=grad_grouped[(b, o, g)][:].rearrange("p c t -> p (c t)"),
+                in_=grad_grouped[piece][:].rearrange("p c t -> p (c t)"),
             )
-            grad_codes[(b, o, g)] = codes
-            grad_scales[(b, o, g)] = scales
+            grad_codes[piece] = codes
+            grad_scales[piece] = scales
 
-        weights_t = {}
-        attention_t, products, product_codes, product_scales, unit_sums = {}, {}, {}, {}, {}
+        weights_t, attention_t, products, product_codes, product_scales, tile_sums = {}, {}, {}, {}, {}, {}
 
         def flip_rows(rows, grouped):
             words = rows.bitcast(F32)
             bank = flipped.tile([P, FLIPS, P], F32, name="bank")
             for j in range(FLIPS):
-                nc.tensor.transpose(bank[:, j, :], words[:, j * WORDS : (j + 1) * WORDS], identity[:])
+                nc.tensor.transpose(bank[:, j, :], words[:, j * P : (j + 1) * P], identity[:])
             nc.scalar.copy(
                 out=grouped.bitcast(F32).rearrange("p (g n u) -> p g n u", g=PASSES, u=2),
                 in_=bank[:].rearrange("p (g u) n -> p g n u", u=2),
             )
 
-        def flip(unit):
-            b, i = divmod(unit, ROW_TILES)
-            c, r = divmod(i, CHUNK)
-            if b == 0:
-                weights_t[i] = keep.tile([P, ORDERS * NODES], BF16, name="weights_t_%d" % i)
-                flip_rows(supports_raw[c][:, r, :], weights_t[i][:, :NODES])
-                flip_rows(cheb_2_raw[c][:, r, :], weights_t[i][:, NODES:])
-            attention_t[unit] = stage.tile([P, NODES], BF16, name="attention_t")
-            flip_rows(attention_raw[b][c][:, r, :], attention_t[unit][:])
+        def flip(i):
+            weights_t[i] = stage.tile([P, ORDERS, NODES], BF16, name="weights_t")
+            attention_t[i] = stage.tile([P, SAMPLES, NODES], BF16, name="attention_t")
+            flip_rows(supports_raw[i][:], weights_t[i][:, 0, :])
+            flip_rows(cheb_2_raw[i][:], weights_t[i][:, 1, :])
+            for b in range(SAMPLES):
+                flip_rows(attention_raw[(b, i)][:], attention_t[i][:, b, :])
 
-        def multiply(unit):
-            i = unit % ROW_TILES
-            products[unit] = stage.tile([P, ORDERS * NODES], BF16, name="products", align_bytes=64)
+        def multiply(i):
+            shape = [P, SAMPLES, ORDERS, NODES]
+            products[i] = stage.tile(shape, BF16, name="products", bufs=3, align_bytes=64)
             nc.vector.tensor_tensor(
-                out=products[unit][:].rearrange("p (o k) -> p o k", o=ORDERS),
-                in0=weights_t[i][:].rearrange("p (o k) -> p o k", o=ORDERS),
-                in1=attention_t[unit][:].unsqueeze(1).to_broadcast([P, ORDERS, NODES]),
+                out=products[i][:],
+                in0=weights_t[i][:].unsqueeze(1).to_broadcast(shape),
+                in1=attention_t[i][:].unsqueeze(2).to_broadcast(shape),
                 op=MULT,
             )
 
-        def quantise(unit):
-            product_codes[unit] = stage.tile([P, ORDERS * PASSES * P], U32, name="product_codes", align_bytes=64)
-            product_scales[unit] = stage.tile([P, ORDERS * PASSES * P], U8, name="product_scales", align_bytes=64)
+        def quantise(i):
+            product_codes[i] = stage.tile([P, len(pieces) * P], U32, name="product_codes", bufs=3, align_bytes=64)
+            product_scales[i] = stage.tile([P, len(pieces) * P], U8, name="product_scales", bufs=3, align_bytes=64)
             nc.vector.quantize_mx(
-                out=product_codes[unit][:].bitcast(E4M3_X4),
-                scales=product_scales[unit][:],
-                in_=products[unit][:],
+                out=product_codes[i][:].bitcast(E4M3_X4),
+                scales=product_scales[i][:],
+                in_=products[i][:].rearrange("p b o k -> p (b o k)"),
             )
 
-        def contract(unit):
-            b = unit // ROW_TILES
-            unit_sums[unit] = sums.tile([P, CHANNELS], F32, name="unit_sums")
-            for index, (o, g) in enumerate(pieces):
+        def contract(i):
+            last = ORDERS * PASSES - 1
+            for index, piece in enumerate(pieces):
+                b = piece[0]
+                if index % (last + 1) == 0:
+                    tile_sums[(b, i)] = sums.tile([P, CHANNELS], F32, name="tile_sums")
                 n_cols = slice(index * P, (index + 1) * P)
                 nc.tensor.matmul_mx(
-                    out=unit_sums[unit][:],
-                    lhsT=product_codes[unit][:, n_cols].bitcast(E4M3_X4),
-                    lhsT_scale=product_scales[unit][:, n_cols],
-                    rhs=grad_codes[(b, o, g)][:].bitcast(E5M2_X4),
-                    rhs_scale=grad_scales[(b, o, g)][:],
-                    start=(index == 0),
-                    stop=(index == len(pieces) - 1),
+                    out=tile_sums[(b, i)][:],
+                    lhsT=product_codes[i][:, n_cols].bitcast(E4M3_X4),
+                    lhsT_scale=product_scales[i][:, n_cols],
+                    rhs=grad_codes[piece][:].bitcast(E5M2_X4),
+                    rhs_scale=grad_scales[piece][:],
+                    start=(index % (last + 1) == 0),
+                    stop=(index % (last + 1) == last),
                 )
 
-        def finish(unit):
-            b, i = divmod(unit, ROW_TILES)
-            c, r = divmod(i, CHUNK)
-            result = results.tile([P, CHANNELS], F32, name="result")
-            nc.vector.scalar_tensor_tensor(
-                out=result[:],
-                in0=grad_0_raw[b][c][:, r, :],
-                scalar=diagonal[:, b, i : i + 1],
-                in1=unit_sums[unit][:],
-                op0=MULT,
-                op1=ADD,
-            )
-            nc.sync.dma_start(out=out_v[b][:, i, :], in_=result[:])
+        def finish(i):
+            for b in range(SAMPLES):
+                result = results.tile([P, CHANNELS], F32, name="result")
+                nc.vector.scalar_tensor_tensor(
+                    out=result[:],
+                    in0=grad_0_raw[i][:, b, :],
+                    scalar=diagonal[:, b, i : i + 1],
+                    in1=tile_sums[(b, i)][:],
+                    op0=MULT,
+                    op1=ADD,
+                )
+                nc.sync.dma_start(out=out_v[b, i], in_=result[:])
 
-        for index, (o, g) in enumerate(pieces):
-            regroup_grad_piece(0, o, g)
-            if index > 0:
-                quantise_grad_piece(0, *pieces[index - 1])
         flip(0)
-        quantise_grad_piece(0, *pieces[-1])
-
-        for s in range(UNITS + 2):
-            if s + 1 < UNITS:
-                flip(s + 1)
-            if 1 <= s <= UNITS:
-                quantise(s - 1)
-                contract(s - 1)
-            if s < UNITS:
+        for s in range(ROW_TILES + FINISH_LAG):
+            if s < ROW_TILES:
                 multiply(s)
-            if s >= 2:
-                finish(s - 2)
-            if s < ROW_TILES and s % CHUNK == 0:
-                regroup_grad_piece(1, *pieces[s // CHUNK])
-            if s < ROW_TILES and s % CHUNK == 1:
-                quantise_grad_piece(1, *pieces[s // CHUNK])
+            if 1 <= s <= ROW_TILES:
+                quantise(s - 1)
+            if s == TILES_BEFORE_GRAD - 1:
+                for index, piece in enumerate(pieces):
+                    regroup_grad_piece(piece)
+                    if index > 0:
+                        quantise_grad_piece(pieces[index - 1])
+                quantise_grad_piece(pieces[-1])
+            if s + 1 < ROW_TILES:
+                flip(s + 1)
+            if 1 <= s <= ROW_TILES:
+                contract(s - 1)
+            if s >= FINISH_LAG:
+                finish(s - FINISH_LAG)

@@ -22,9 +22,9 @@ PASSES = NODES // (P * PACK)
 ROW_TILES = NODES // P
 FLIPS = NODES // (2 * P)
 
-TILES_BEFORE_GRAD = 2
-FINISH_LAG = 2
-VECTOR_COLUMNS = 256
+PIECES_A_STEP = 2
+CATCH_UP = 2
+VECTOR_COLUMNS = (128, 0)
 
 FLOPS = 2 * SAMPLES * ORDERS * NODES * NODES * CHANNELS
 BYTES = 2 * (2 * NODES * NODES + SAMPLES * NODES * NODES + 3 * SAMPLES * NODES * CHANNELS) + 4 * SAMPLES * NODES * CHANNELS
@@ -46,10 +46,11 @@ def tile_napl_conv_withsat_pb_kernel(tc, supports, cheb_2, spatial_attention, x,
         keep = stack.enter_context(tc.tile_pool(name="keep", bufs=1))
         stage = stack.enter_context(tc.tile_pool(name="stage", bufs=2))
         results = stack.enter_context(tc.tile_pool(name="results", bufs=10))
-        flipped = stack.enter_context(tc.psum_pool(name="flipped", bufs=4))
+        flipped = stack.enter_context(tc.psum_pool(name="flipped", bufs=2))
         sums = stack.enter_context(tc.psum_pool(name="sums", bufs=4))
 
         pieces = [(b, o, g) for b in range(SAMPLES) for o in range(ORDERS) for g in range(PASSES)]
+        pieces_a_sample = ORDERS * PASSES
         supports_raw, cheb_2_raw, attention_raw, grad_0_raw, grad_raw = {}, {}, {}, {}, {}
 
         def load_rows(view, name):
@@ -75,17 +76,24 @@ def tile_napl_conv_withsat_pb_kernel(tc, supports, cheb_2, spatial_attention, x,
 
         diagonal_bf16 = [keep.tile([P, ROW_TILES], BF16, name="diagonal_bf16_%d" % b) for b in range(SAMPLES)]
 
-        for i in range(TILES_BEFORE_GRAD):
-            load_matrices(i)
-        for piece in pieces:
-            load_grad_piece(*piece)
-        with nc.allow_non_contiguous_dma(reason="2,048 diagonal elements, one to a row of the attention"):
-            for b in range(SAMPLES):
-                nc.sync.dma_start(out=diagonal_bf16[b][:], in_=diagonal_v[b].rearrange("(i p) -> p i", p=P))
-        for i in range(TILES_BEFORE_GRAD, ROW_TILES + FINISH_LAG):
-            if i < ROW_TILES:
-                load_matrices(i)
-            load_grad_0(i - FINISH_LAG)
+        def load_diagonal():
+            with nc.allow_non_contiguous_dma(reason="2,048 diagonal elements, one to a row of the attention"):
+                for b in range(SAMPLES):
+                    nc.sync.dma_start(out=diagonal_bf16[b][:], in_=diagonal_v[b].rearrange("(i p) -> p i", p=P))
+
+        def pieces_of_step(s):
+            return pieces[s * PIECES_A_STEP : (s + 1) * PIECES_A_STEP]
+
+        load_matrices(0)
+        for s in range(ROW_TILES + 1):
+            for piece in pieces_of_step(s):
+                load_grad_piece(*piece)
+            if s + 1 < ROW_TILES:
+                load_matrices(s + 1)
+            if s == 1:
+                load_diagonal()
+            if s >= 1:
+                load_grad_0(s - 1)
 
         identity = keep.tile([P, P], F32)
         make_identity(nc, identity[:])
@@ -98,13 +106,15 @@ def tile_napl_conv_withsat_pb_kernel(tc, supports, cheb_2, spatial_attention, x,
         def regroup_grad_piece(piece):
             raw = grad_raw[piece]
             grouped = stage.tile([P, CHANNELS, PACK], BF16, name="grad_grouped", bufs=3, align_bytes=64)
-            nc.vector.tensor_copy(
-                out=grouped[:, :VECTOR_COLUMNS, :].rearrange("p (c i) t -> p c t i", i=4),
-                in_=raw[:, :, :VECTOR_COLUMNS].rearrange("p t (c i) -> p c t i", i=4),
-            )
+            split = VECTOR_COLUMNS[piece[0]]
+            if split:
+                nc.vector.tensor_copy(
+                    out=grouped[:, :split, :].rearrange("p (c i) t -> p c t i", i=4),
+                    in_=raw[:, :, :split].rearrange("p t (c i) -> p c t i", i=4),
+                )
             nc.scalar.copy(
-                out=grouped[:, VECTOR_COLUMNS:, :].rearrange("p (c i) t -> p c t i", i=4),
-                in_=raw[:, :, VECTOR_COLUMNS:].rearrange("p t (c i) -> p c t i", i=4),
+                out=grouped[:, split:, :].rearrange("p (c i) t -> p c t i", i=4),
+                in_=raw[:, :, split:].rearrange("p t (c i) -> p c t i", i=4),
             )
             grad_grouped[piece] = grouped
 
@@ -119,90 +129,97 @@ def tile_napl_conv_withsat_pb_kernel(tc, supports, cheb_2, spatial_attention, x,
             grad_codes[piece] = codes
             grad_scales[piece] = scales
 
-        weights_t, attention_t, products, product_codes, product_scales, tile_sums = {}, {}, {}, {}, {}, {}
-
-        def flip_rows(rows, grouped):
-            words = rows.bitcast(F32)
-            bank = flipped.tile([P, FLIPS, P], F32, name="bank")
-            for j in range(FLIPS):
-                nc.tensor.transpose(bank[:, j, :], words[:, j * P : (j + 1) * P], identity[:])
-            nc.scalar.copy(
-                out=grouped.bitcast(F32).rearrange("p (g n u) -> p g n u", g=PASSES, u=2),
-                in_=bank[:].rearrange("p (g u) n -> p g n u", u=2),
-            )
+        weights_t, attention_t, products, product_codes, product_scales, unit_sums = {}, {}, {}, {}, {}, {}
 
         def flip(i):
             weights_t[i] = stage.tile([P, ORDERS, NODES], BF16, name="weights_t")
-            attention_t[i] = stage.tile([P, SAMPLES, NODES], BF16, name="attention_t")
-            flip_rows(supports_raw[i][:], weights_t[i][:, 0, :])
-            flip_rows(cheb_2_raw[i][:], weights_t[i][:, 1, :])
+            for o, raw in enumerate((supports_raw[i], cheb_2_raw[i])):
+                bank = flipped.tile([P, FLIPS, P], F32, name="weights_bank")
+                for j in range(FLIPS):
+                    nc.tensor.transpose(bank[:, j, :], raw[:].bitcast(F32)[:, j * P : (j + 1) * P], identity[:])
+                nc.scalar.copy(
+                    out=weights_t[i][:, o, :].bitcast(F32).rearrange("p (g n u) -> p g n u", g=PASSES, u=2),
+                    in_=bank[:].rearrange("p (g u) n -> p g n u", u=2),
+                )
             for b in range(SAMPLES):
-                flip_rows(attention_raw[(b, i)][:], attention_t[i][:, b, :])
+                bank = flipped.tile([P, PASSES, P, 2], F32, name="attention_bank")
+                for j in range(FLIPS):
+                    g, u = divmod(j, 2)
+                    nc.tensor.transpose(bank[:, g, :, u], attention_raw[(b, i)][:].bitcast(F32)[:, j * P : (j + 1) * P], identity[:])
+                attention_t[(b, i)] = bank
 
         def multiply(i):
-            shape = [P, SAMPLES, ORDERS, NODES]
-            products[i] = stage.tile(shape, BF16, name="products", bufs=3, align_bytes=64)
-            nc.vector.tensor_tensor(
-                out=products[i][:],
-                in0=weights_t[i][:].unsqueeze(1).to_broadcast(shape),
-                in1=attention_t[i][:].unsqueeze(2).to_broadcast(shape),
-                op=MULT,
-            )
+            products[i] = stage.tile([P, SAMPLES, ORDERS, NODES], BF16, name="products", align_bytes=64)
+            for b in range(SAMPLES):
+                attention_bf16 = attention_t[(b, i)][:].rearrange("p g n u -> p (g n u)").bitcast(BF16)
+                nc.vector.tensor_tensor(
+                    out=products[i][:, b],
+                    in0=weights_t[i][:],
+                    in1=attention_bf16.unsqueeze(1).to_broadcast([P, ORDERS, NODES]),
+                    op=MULT,
+                )
 
         def quantise(i):
-            product_codes[i] = stage.tile([P, len(pieces) * P], U32, name="product_codes", bufs=3, align_bytes=64)
-            product_scales[i] = stage.tile([P, len(pieces) * P], U8, name="product_scales", bufs=3, align_bytes=64)
+            product_codes[i] = stage.tile([P, len(pieces) * P], U32, name="product_codes", bufs=5, align_bytes=64)
+            product_scales[i] = stage.tile([P, len(pieces) * P], U8, name="product_scales", bufs=5, align_bytes=64)
             nc.vector.quantize_mx(
                 out=product_codes[i][:].bitcast(E4M3_X4),
                 scales=product_scales[i][:],
                 in_=products[i][:].rearrange("p b o k -> p (b o k)"),
             )
 
-        def contract(i):
-            last = ORDERS * PASSES - 1
-            for index, piece in enumerate(pieces):
-                b = piece[0]
-                if index % (last + 1) == 0:
-                    tile_sums[(b, i)] = sums.tile([P, CHANNELS], F32, name="tile_sums")
-                n_cols = slice(index * P, (index + 1) * P)
+        def contract(i, b):
+            unit_sums[(i, b)] = sums.tile([P, CHANNELS], F32, name="unit_sums")
+            for index in range(pieces_a_sample):
+                piece = pieces[b * pieces_a_sample + index]
+                n_cols = slice((b * pieces_a_sample + index) * P, (b * pieces_a_sample + index + 1) * P)
                 nc.tensor.matmul_mx(
-                    out=tile_sums[(b, i)][:],
+                    out=unit_sums[(i, b)][:],
                     lhsT=product_codes[i][:, n_cols].bitcast(E4M3_X4),
                     lhsT_scale=product_scales[i][:, n_cols],
                     rhs=grad_codes[piece][:].bitcast(E5M2_X4),
                     rhs_scale=grad_scales[piece][:],
-                    start=(index % (last + 1) == 0),
-                    stop=(index % (last + 1) == last),
+                    start=(index == 0),
+                    stop=(index == pieces_a_sample - 1),
                 )
 
-        def finish(i):
-            for b in range(SAMPLES):
+        def finish(units):
+            for i, b in units:
                 result = results.tile([P, CHANNELS], F32, name="result")
                 nc.vector.scalar_tensor_tensor(
                     out=result[:],
                     in0=grad_0_raw[i][:, b, :],
                     scalar=diagonal[:, b, i : i + 1],
-                    in1=tile_sums[(b, i)][:],
+                    in1=unit_sums[(i, b)][:],
                     op0=MULT,
                     op1=ADD,
                 )
                 nc.sync.dma_start(out=out_v[b, i], in_=result[:])
 
+        waiting = [[] for b in range(SAMPLES)]
+        contracted = []
         flip(0)
-        for s in range(ROW_TILES + FINISH_LAG):
+        for s in range(ROW_TILES + 1):
+            last_tile = s == ROW_TILES - 1
             if s < ROW_TILES:
                 multiply(s)
-            if 1 <= s <= ROW_TILES:
-                quantise(s - 1)
-            if s == TILES_BEFORE_GRAD - 1:
-                for index, piece in enumerate(pieces):
-                    regroup_grad_piece(piece)
-                    if index > 0:
-                        quantise_grad_piece(pieces[index - 1])
-                quantise_grad_piece(pieces[-1])
+            for piece in pieces_of_step(s):
+                regroup_grad_piece(piece)
             if s + 1 < ROW_TILES:
                 flip(s + 1)
-            if 1 <= s <= ROW_TILES:
-                contract(s - 1)
-            if s >= FINISH_LAG:
-                finish(s - FINISH_LAG)
+            if last_tile:
+                quantise(s)
+            finish(contracted)
+            contracted = []
+            if s < ROW_TILES and not last_tile:
+                quantise(s)
+            for piece in pieces_of_step(s):
+                quantise_grad_piece(piece)
+            for b in range(SAMPLES):
+                if s < ROW_TILES:
+                    waiting[b].append(s)
+                if (s + 1) * PIECES_A_STEP >= (b + 1) * pieces_a_sample:
+                    for i in waiting[b][:CATCH_UP]:
+                        contract(i, b)
+                        contracted.append((i, b))
+                    waiting[b] = waiting[b][CATCH_UP:]

@@ -11,6 +11,7 @@ E4M3_X4 = mybir.dt.float8_e4m3fn_x4
 E5M2_X4 = mybir.dt.float8_e5m2_x4
 MULT = mybir.AluOpType.mult
 ADD = mybir.AluOpType.add
+COPY = mybir.ActivationFunctionType.Copy
 
 P = 128
 SAMPLES = 2
@@ -39,7 +40,6 @@ def tile_napl_conv_withsat_pb_kernel(tc, supports, cheb_2, spatial_attention, x,
     grad_v = grad_out.rearrange("k b m f t -> k b m (f t)")
     grad_0_v = grad_v[0].rearrange("b (i p) c -> i p b c", p=P)
     out_v = out.rearrange("b (i p) f t -> b i p (f t)", p=P)
-    diagonal_v = spatial_attention.rearrange("b n m -> b (n m)")[:, 0 : NODES * NODES : NODES + 1]
 
     with ExitStack() as stack:
         stack.enter_context(tc.manual_schedule())
@@ -60,9 +60,9 @@ def tile_napl_conv_withsat_pb_kernel(tc, supports, cheb_2, spatial_attention, x,
 
         def load_matrices(i):
             supports_raw[i] = load_rows(supports_v[i], "supports_raw_%d" % i)
+            attention_raw[(0, i)] = load_rows(attention_v[0, i], "attention_raw_%d_%d" % (0, i))
             cheb_2_raw[i] = load_rows(cheb_2_v[i], "cheb_2_raw_%d" % i)
-            for b in range(SAMPLES):
-                attention_raw[(b, i)] = load_rows(attention_v[b, i], "attention_raw_%d_%d" % (b, i))
+            attention_raw[(1, i)] = load_rows(attention_v[1, i], "attention_raw_%d_%d" % (1, i))
 
         def load_grad_0(i):
             grad_0_raw[i] = keep.tile([P, SAMPLES, CHANNELS], BF16, name="grad_0_raw_%d" % i)
@@ -74,13 +74,6 @@ def tile_napl_conv_withsat_pb_kernel(tc, supports, cheb_2, spatial_attention, x,
             nc.sync.dma_start(out=raw[:].rearrange("p (u e) c -> p u (e c)", u=2), in_=rows[g])
             grad_raw[(b, o, g)] = raw
 
-        diagonal_bf16 = [keep.tile([P, ROW_TILES], BF16, name="diagonal_bf16_%d" % b) for b in range(SAMPLES)]
-
-        def load_diagonal():
-            with nc.allow_non_contiguous_dma(reason="2,048 diagonal elements, one to a row of the attention"):
-                for b in range(SAMPLES):
-                    nc.sync.dma_start(out=diagonal_bf16[b][:], in_=diagonal_v[b].rearrange("(i p) -> p i", p=P))
-
         def pieces_of_step(s):
             return pieces[s * PIECES_A_STEP : (s + 1) * PIECES_A_STEP]
 
@@ -90,16 +83,21 @@ def tile_napl_conv_withsat_pb_kernel(tc, supports, cheb_2, spatial_attention, x,
                 load_grad_piece(*piece)
             if s + 1 < ROW_TILES:
                 load_matrices(s + 1)
-            if s == 1:
-                load_diagonal()
             if s >= 1:
                 load_grad_0(s - 1)
 
         identity = keep.tile([P, P], F32)
         make_identity(nc, identity[:])
+        identity_bf16 = keep.tile([P, P], BF16)
+        make_identity(nc, identity_bf16[:])
         diagonal = keep.tile([P, SAMPLES, ROW_TILES], F32)
-        for b in range(SAMPLES):
-            nc.gpsimd.tensor_copy(out=diagonal[:, b, :], in_=diagonal_bf16[b][:])
+
+        def pick_diagonal(i):
+            for b in range(SAMPLES):
+                masked = stage.tile([P, P], BF16, name="masked")
+                nc.gpsimd.tensor_tensor(out=masked[:], in0=attention_raw[(b, i)][:, i * P : (i + 1) * P], in1=identity_bf16[:], op=MULT)
+                unused = stage.tile([P, P], BF16, name="unused")
+                nc.scalar.activation(out=unused[:], in_=masked[:], func=COPY, accum_out=diagonal[:, b, i : i + 1])
 
         grad_grouped, grad_codes, grad_scales = {}, {}, {}
 
@@ -133,7 +131,9 @@ def tile_napl_conv_withsat_pb_kernel(tc, supports, cheb_2, spatial_attention, x,
 
         def flip(i):
             weights_t[i] = stage.tile([P, ORDERS, NODES], BF16, name="weights_t")
-            for o, raw in enumerate((supports_raw[i], cheb_2_raw[i])):
+
+            def flip_weights(o):
+                raw = (supports_raw[i], cheb_2_raw[i])[o]
                 bank = flipped.tile([P, FLIPS, P], F32, name="weights_bank")
                 for j in range(FLIPS):
                     nc.tensor.transpose(bank[:, j, :], raw[:].bitcast(F32)[:, j * P : (j + 1) * P], identity[:])
@@ -141,17 +141,34 @@ def tile_napl_conv_withsat_pb_kernel(tc, supports, cheb_2, spatial_attention, x,
                     out=weights_t[i][:, o, :].bitcast(F32).rearrange("p (g n u) -> p g n u", g=PASSES, u=2),
                     in_=bank[:].rearrange("p (g u) n -> p g n u", u=2),
                 )
-            for b in range(SAMPLES):
+
+            def flip_attention(b):
                 bank = flipped.tile([P, PASSES, P, 2], F32, name="attention_bank")
                 for j in range(FLIPS):
                     g, u = divmod(j, 2)
                     nc.tensor.transpose(bank[:, g, :, u], attention_raw[(b, i)][:].bitcast(F32)[:, j * P : (j + 1) * P], identity[:])
                 attention_t[(b, i)] = bank
 
+            if i == 0:
+                flip_weights(0)
+                flip_attention(0)
+                flip_weights(1)
+                flip_attention(1)
+            else:
+                flip_weights(0)
+                flip_weights(1)
+                flip_attention(0)
+                flip_attention(1)
+            pick_diagonal(i)
+
         def multiply(i):
             products[i] = stage.tile([P, SAMPLES, ORDERS, NODES], BF16, name="products", align_bytes=64)
             for b in range(SAMPLES):
                 attention_bf16 = attention_t[(b, i)][:].rearrange("p g n u -> p (g n u)").bitcast(BF16)
+                if i == 0 and b == 0:
+                    for o in range(ORDERS):
+                        nc.vector.tensor_tensor(out=products[i][:, b, o], in0=weights_t[i][:, o], in1=attention_bf16, op=MULT)
+                    continue
                 nc.vector.tensor_tensor(
                     out=products[i][:, b],
                     in0=weights_t[i][:],

@@ -185,6 +185,17 @@ def tile_napl_conv_withsat_pb_kernel(tc, supports, cheb_2, spatial_attention, x,
                 in_=products[i][:].rearrange("p b o k -> p (b o k)"),
             )
 
+        def quantise_sample(i, b):
+            if b == 0:
+                product_codes[i] = stage.tile([P, len(pieces) * P], U32, name="product_codes", bufs=5, align_bytes=64)
+                product_scales[i] = stage.tile([P, len(pieces) * P], U8, name="product_scales", bufs=5, align_bytes=64)
+            cols = slice(b * pieces_a_sample * P, (b + 1) * pieces_a_sample * P)
+            nc.vector.quantize_mx(
+                out=product_codes[i][:, cols].bitcast(E4M3_X4),
+                scales=product_scales[i][:, cols],
+                in_=products[i][:, b].rearrange("p o k -> p (o k)"),
+            )
+
         def contract(i, b):
             unit_sums[(i, b)] = sums.tile([P, CHANNELS], F32, name="unit_sums")
             for index in range(pieces_a_sample):
@@ -225,11 +236,14 @@ def tile_napl_conv_withsat_pb_kernel(tc, supports, cheb_2, spatial_attention, x,
             if s + 1 < ROW_TILES:
                 flip(s + 1)
             if last_tile:
-                quantise(s)
-            finish(contracted)
-            contracted = []
+                for b in range(SAMPLES):
+                    quantise_sample(s, b)
+            held_back = 1 if (s < ROW_TILES and not last_tile and len(contracted) > 1) else 0
+            finish(contracted[: len(contracted) - held_back])
             if s < ROW_TILES and not last_tile:
                 quantise(s)
+            finish(contracted[len(contracted) - held_back :])
+            contracted = []
             for piece in pieces_of_step(s):
                 quantise_grad_piece(piece)
             for b in range(SAMPLES):

@@ -11,7 +11,6 @@ E4M3_X4 = mybir.dt.float8_e4m3fn_x4
 E5M2_X4 = mybir.dt.float8_e5m2_x4
 MULT = mybir.AluOpType.mult
 ADD = mybir.AluOpType.add
-COPY = mybir.ActivationFunctionType.Copy
 
 P = 128
 SAMPLES = 2
@@ -40,6 +39,7 @@ def tile_napl_conv_withsat_pb_kernel(tc, supports, cheb_2, spatial_attention, x,
     grad_v = grad_out.rearrange("k b m f t -> k b m (f t)")
     grad_0_v = grad_v[0].rearrange("b (i p) c -> i p b c", p=P)
     out_v = out.rearrange("b (i p) f t -> b i p (f t)", p=P)
+    diagonal_v = spatial_attention.rearrange("b n m -> b (n m)")[:, 0 : NODES * NODES : NODES + 1].rearrange("b (i p) -> b p i", p=P)
 
     with ExitStack() as stack:
         stack.enter_context(tc.manual_schedule())
@@ -74,6 +74,14 @@ def tile_napl_conv_withsat_pb_kernel(tc, supports, cheb_2, spatial_attention, x,
             nc.sync.dma_start(out=raw[:].rearrange("p (u e) c -> p u (e c)", u=2), in_=rows[g])
             grad_raw[(b, o, g)] = raw
 
+        half_tiles = ROW_TILES // 2
+        diagonal = {}
+
+        def load_diagonal(b, h):
+            diagonal[(b, h)] = keep.tile([P, half_tiles], BF16, name="diagonal_%d_%d" % (b, h))
+            with nc.allow_non_contiguous_dma(reason="512 diagonal elements, one to a row of the attention"):
+                nc.sync.dma_start(out=diagonal[(b, h)][:], in_=diagonal_v[b][:, h * half_tiles : (h + 1) * half_tiles])
+
         def pieces_of_step(s):
             return pieces[s * PIECES_A_STEP : (s + 1) * PIECES_A_STEP]
 
@@ -83,22 +91,18 @@ def tile_napl_conv_withsat_pb_kernel(tc, supports, cheb_2, spatial_attention, x,
                 load_grad_piece(*piece)
             if s + 1 < ROW_TILES:
                 load_matrices(s + 1)
+            if s == 1:
+                load_diagonal(0, 0)
+            if s == 3:
+                load_diagonal(1, 0)
+            if s == 4:
+                load_diagonal(0, 1)
+                load_diagonal(1, 1)
             if s >= 1:
                 load_grad_0(s - 1)
 
         identity = keep.tile([P, P], F32)
         make_identity(nc, identity[:])
-        identity_bf16 = keep.tile([P, P], BF16)
-        make_identity(nc, identity_bf16[:])
-        diagonal = keep.tile([P, SAMPLES, ROW_TILES], F32)
-
-        def pick_diagonal(i):
-            for b in range(SAMPLES):
-                masked = stage.tile([P, P], BF16, name="masked")
-                nc.gpsimd.tensor_tensor(out=masked[:], in0=attention_raw[(b, i)][:, i * P : (i + 1) * P], in1=identity_bf16[:], op=MULT)
-                unused = stage.tile([P, P], BF16, name="unused")
-                nc.scalar.activation(out=unused[:], in_=masked[:], func=COPY, accum_out=diagonal[:, b, i : i + 1])
-
         grad_grouped, grad_codes, grad_scales = {}, {}, {}
 
         def regroup_grad_piece(piece):
@@ -159,7 +163,6 @@ def tile_napl_conv_withsat_pb_kernel(tc, supports, cheb_2, spatial_attention, x,
                 flip_weights(1)
                 flip_attention(0)
                 flip_attention(1)
-            pick_diagonal(i)
 
         def multiply(i):
             products[i] = stage.tile([P, SAMPLES, ORDERS, NODES], BF16, name="products", align_bytes=64)
@@ -217,7 +220,7 @@ def tile_napl_conv_withsat_pb_kernel(tc, supports, cheb_2, spatial_attention, x,
                 nc.vector.scalar_tensor_tensor(
                     out=result[:],
                     in0=grad_0_raw[i][:, b, :],
-                    scalar=diagonal[:, b, i : i + 1],
+                    scalar=diagonal[(b, i // half_tiles)][:, i % half_tiles : i % half_tiles + 1],
                     in1=unit_sums[(i, b)][:],
                     op0=MULT,
                     op1=ADD,

@@ -37,7 +37,7 @@ def tile_napl_conv_withsat_pb_kernel(tc, supports, cheb_2, spatial_attention, x,
     cheb_2_v = cheb_2.rearrange("(i p) m -> i p m", p=P)
     attention_v = spatial_attention.rearrange("b (i p) m -> b i p m", p=P)
     grad_v = grad_out.rearrange("k b m f t -> k b m (f t)")
-    grad_0_v = grad_v[0].rearrange("b (i p) c -> i p b c", p=P)
+    grad_0_v = grad_v[0].rearrange("b (i p) c -> b i p c", p=P)
     out_v = out.rearrange("b (i p) f t -> b i p (f t)", p=P)
     diagonal_v = spatial_attention.rearrange("b n m -> b (n m)")[:, 0 : NODES * NODES : NODES + 1].rearrange("b (i p) -> b p i", p=P)
 
@@ -64,9 +64,9 @@ def tile_napl_conv_withsat_pb_kernel(tc, supports, cheb_2, spatial_attention, x,
             cheb_2_raw[i] = load_rows(cheb_2_v[i], "cheb_2_raw_%d" % i)
             attention_raw[(1, i)] = load_rows(attention_v[1, i], "attention_raw_%d_%d" % (1, i))
 
-        def load_grad_0(i):
-            grad_0_raw[i] = keep.tile([P, SAMPLES, CHANNELS], BF16, name="grad_0_raw_%d" % i)
-            nc.sync.dma_start(out=grad_0_raw[i][:], in_=grad_0_v[i])
+        def load_grad_0(i, b):
+            grad_0_raw[(i, b)] = keep.tile([P, CHANNELS], BF16, name="grad_0_raw_%d_%d" % (i, b))
+            nc.sync.dma_start(out=grad_0_raw[(i, b)][:], in_=grad_0_v[b, i])
 
         def load_grad_piece(b, o, g):
             raw = keep.tile([P, PACK, CHANNELS], BF16, name="grad_raw_%d_%d_%d" % (b, o, g))
@@ -99,7 +99,11 @@ def tile_napl_conv_withsat_pb_kernel(tc, supports, cheb_2, spatial_attention, x,
                 load_diagonal(0, 1)
                 load_diagonal(1, 1)
             if s >= 1:
-                load_grad_0(s - 1)
+                load_grad_0(s - 1, 0)
+            if s >= 3:
+                for i in (2 * (s - 3), 2 * (s - 3) + 1):
+                    if i < ROW_TILES:
+                        load_grad_0(i, 1)
 
         identity = keep.tile([P, P], F32)
         make_identity(nc, identity[:])
@@ -219,7 +223,7 @@ def tile_napl_conv_withsat_pb_kernel(tc, supports, cheb_2, spatial_attention, x,
                 result = results.tile([P, CHANNELS], F32, name="result")
                 nc.vector.scalar_tensor_tensor(
                     out=result[:],
-                    in0=grad_0_raw[i][:, b, :],
+                    in0=grad_0_raw[(i, b)][:],
                     scalar=diagonal[(b, i // half_tiles)][:, i % half_tiles : i % half_tiles + 1],
                     in1=unit_sums[(i, b)][:],
                     op0=MULT,

@@ -25,6 +25,7 @@ FLIPS = NODES // (2 * P)
 PIECES_A_STEP = 2
 CATCH_UP = 2
 VECTOR_COLUMNS = (128, 0)
+PE_PIECES = (5, 7)
 
 FLOPS = 2 * SAMPLES * ORDERS * NODES * NODES * CHANNELS
 BYTES = 2 * (2 * NODES * NODES + SAMPLES * NODES * NODES + 3 * SAMPLES * NODES * CHANNELS) + 4 * SAMPLES * NODES * CHANNELS
@@ -93,13 +94,14 @@ def tile_napl_conv_withsat_pb_kernel(tc, supports, cheb_2, spatial_attention, x,
                 load_matrices(s + 1)
             if s == 1:
                 load_diagonal(0, 0)
+                load_grad_0(0, 0)
             if s == 3:
                 load_diagonal(1, 0)
             if s == 4:
                 load_diagonal(0, 1)
                 load_diagonal(1, 1)
-            if s >= 1:
-                load_grad_0(s - 1, 0)
+            if 1 <= s < ROW_TILES:
+                load_grad_0(s, 0)
             if s >= 3:
                 for i in (2 * (s - 3), 2 * (s - 3) + 1):
                     if i < ROW_TILES:
@@ -107,11 +109,29 @@ def tile_napl_conv_withsat_pb_kernel(tc, supports, cheb_2, spatial_attention, x,
 
         identity = keep.tile([P, P], F32)
         make_identity(nc, identity[:])
+        identity_bf16 = keep.tile([P, P], BF16)
+        make_identity(nc, identity_bf16[:])
         grad_grouped, grad_codes, grad_scales = {}, {}, {}
 
         def regroup_grad_piece(piece):
             raw = grad_raw[piece]
             grouped = stage.tile([P, CHANNELS, PACK], BF16, name="grad_grouped", bufs=3, align_bytes=64)
+            if pieces.index(piece) in PE_PIECES:
+                half = CHANNELS // 2
+                for h in range(2):
+                    bank = sums.tile([P, half, PACK], BF16, name="unit_sums")
+                    for q in range(2):
+                        cols = slice(h * half + q * P, h * half + (q + 1) * P)
+                        nc.tensor.matmul(
+                            out=bank[:, q * P : (q + 1) * P, :].rearrange("p c t -> p (c t)"),
+                            lhsT=identity_bf16[:],
+                            rhs=raw[:, :, cols].rearrange("p t c -> p c t"),
+                            start=True,
+                            stop=True,
+                        )
+                    nc.scalar.copy(out=grouped[:, h * half : (h + 1) * half, :], in_=bank[:])
+                grad_grouped[piece] = grouped
+                return
             split = VECTOR_COLUMNS[piece[0]]
             if split:
                 nc.vector.tensor_copy(

@@ -25,7 +25,7 @@ FLIPS = NODES // (2 * P)
 PIECES_A_STEP = 2
 CATCH_UP = 2
 VECTOR_COLUMNS = (128, 0)
-PE_PIECES = (5, 7)
+PE_PIECES = (1, 3, 5, 7)
 
 FLOPS = 2 * SAMPLES * ORDERS * NODES * NODES * CHANNELS
 BYTES = 2 * (2 * NODES * NODES + SAMPLES * NODES * NODES + 3 * SAMPLES * NODES * CHANNELS) + 4 * SAMPLES * NODES * CHANNELS

@@ -11,6 +11,7 @@ E4M3_X4 = mybir.dt.float8_e4m3fn_x4
 E5M2_X4 = mybir.dt.float8_e5m2_x4
 MULT = mybir.AluOpType.mult
 ADD = mybir.AluOpType.add
+COPY = mybir.ActivationFunctionType.Copy
 
 P = 128
 SAMPLES = 2
@@ -25,6 +26,7 @@ FLIPS = NODES // (2 * P)
 PIECES_A_STEP = 2
 CATCH_UP = 2
 VECTOR_COLUMNS = (128, 0)
+ELSEWHERE = ((1, 1), (3, 1), (5, 1), (6, 1))
 PE_PIECES = (1, 3, 5, 7)
 
 FLOPS = 2 * SAMPLES * ORDERS * NODES * NODES * CHANNELS
@@ -238,6 +240,21 @@ def tile_napl_conv_withsat_pb_kernel(tc, supports, cheb_2, spatial_attention, x,
                     stop=(index == pieces_a_sample - 1),
                 )
 
+        diagonal_f32 = {}
+
+        def finish_elsewhere(i, b):
+            h = i // half_tiles
+            if (b, h) not in diagonal_f32:
+                diagonal_f32[(b, h)] = keep.tile([P, half_tiles], F32, name="diagonal_f32_%d_%d" % (b, h))
+                nc.gpsimd.tensor_copy(out=diagonal_f32[(b, h)][:], in_=diagonal[(b, h)][:])
+            result = results.tile([P, CHANNELS], F32, name="result")
+            first_term = stage.tile([P, CHANNELS], F32, name="first_term")
+            nc.scalar.activation(out=first_term[:], in_=grad_0_raw[(i, b)][:], func=COPY, scale=diagonal_f32[(b, h)][:, i % half_tiles : i % half_tiles + 1])
+            sums_copy = stage.tile([P, CHANNELS], F32, name="sums_copy")
+            nc.scalar.copy(out=sums_copy[:], in_=unit_sums[(i, b)][:])
+            nc.gpsimd.tensor_tensor(out=result[:], in0=first_term[:], in1=sums_copy[:], op=ADD)
+            nc.sync.dma_start(out=out_v[b, i], in_=result[:])
+
         def finish(units):
             for i, b in units:
                 result = results.tile([P, CHANNELS], F32, name="result")
@@ -279,5 +296,8 @@ def tile_napl_conv_withsat_pb_kernel(tc, supports, cheb_2, spatial_attention, x,
                 if (s + 1) * PIECES_A_STEP >= (b + 1) * pieces_a_sample:
                     for i in waiting[b][:CATCH_UP]:
                         contract(i, b)
-                        contracted.append((i, b))
+                        if (i, b) in ELSEWHERE:
+                            finish_elsewhere(i, b)
+                        else:
+                            contracted.append((i, b))
                     waiting[b] = waiting[b][CATCH_UP:]

@@ -25,8 +25,10 @@ FLIPS = NODES // (2 * P)
 
 PIECES_A_STEP = 2
 CATCH_UP = 2
+B1_QUOTA = {3: 2, 4: 1, 5: 1, 6: 2, 7: 2}
+B_ORDER = (1, 0)
 VECTOR_COLUMNS = (128, 0)
-ELSEWHERE = ((1, 1), (3, 1), (5, 1), (6, 1))
+ELSEWHERE = ((1, 1), (2, 1), (3, 1), (5, 1))
 PE_PIECES = (1, 3, 5, 7)
 
 FLOPS = 2 * SAMPLES * ORDERS * NODES * NODES * CHANNELS
@@ -290,14 +292,15 @@ def tile_napl_conv_withsat_pb_kernel(tc, supports, cheb_2, spatial_attention, x,
             contracted = []
             for piece in pieces_of_step(s):
                 quantise_grad_piece(piece)
-            for b in range(SAMPLES):
+            for b in B_ORDER:
                 if s < ROW_TILES:
                     waiting[b].append(s)
                 if (s + 1) * PIECES_A_STEP >= (b + 1) * pieces_a_sample:
-                    for i in waiting[b][:CATCH_UP]:
+                    quota = CATCH_UP if b == 0 else B1_QUOTA.get(s, CATCH_UP)
+                    for i in waiting[b][:quota]:
                         contract(i, b)
                         if (i, b) in ELSEWHERE:
                             finish_elsewhere(i, b)
                         else:
                             contracted.append((i, b))
-                    waiting[b] = waiting[b][CATCH_UP:]
+                    waiting[b] = waiting[b][quota:]

@@ -90,12 +90,7 @@ def tile_napl_conv_withsat_pb_kernel(tc, supports, cheb_2, spatial_attention, x,
         def pieces_of_step(s):
             return pieces[s * PIECES_A_STEP : (s + 1) * PIECES_A_STEP]
 
-        load_matrices(0)
-        for s in range(ROW_TILES + 1):
-            for piece in pieces_of_step(s):
-                load_grad_piece(*piece)
-            if s + 1 < ROW_TILES:
-                load_matrices(s + 1)
+        def load_for_adds(s):
             if s == 1:
                 load_diagonal(0, 0)
                 load_grad_0(0, 0)
@@ -110,6 +105,15 @@ def tile_napl_conv_withsat_pb_kernel(tc, supports, cheb_2, spatial_attention, x,
                 for i in (2 * (s - 3), 2 * (s - 3) + 1):
                     if i < ROW_TILES:
                         load_grad_0(i, 1)
+
+        load_matrices(0)
+        for s in range(ROW_TILES + 1):
+            for piece in pieces_of_step(s):
+                load_grad_piece(*piece)
+            if s >= 1:
+                load_for_adds(s - 1)
+            if s + 1 < ROW_TILES:
+                load_matrices(s + 1)
 
         identity = keep.tile([P, P], F32)
         make_identity(nc, identity[:])

from contextlib import ExitStack

import concourse.mybir as mybir
from concourse.masks import make_identity

BF16 = mybir.dt.bfloat16
F32 = mybir.dt.float32
U32 = mybir.dt.uint32
U8 = mybir.dt.uint8
E4M3_X4 = mybir.dt.float8_e4m3fn_x4
E5M2_X4 = mybir.dt.float8_e5m2_x4
MULT = mybir.AluOpType.mult
ADD = mybir.AluOpType.add
COPY = mybir.ActivationFunctionType.Copy

P = 128
SAMPLES = 2
NODES = 1024
CHANNELS = 512
ORDERS = 2
PACK = 4
PASSES = NODES // (P * PACK)
ROW_TILES = NODES // P
FLIPS = NODES // (2 * P)

PIECES_A_STEP = 2
CATCH_UP = 2
B1_QUOTA = {3: 2, 4: 1, 5: 1, 6: 2, 7: 2}
B_ORDER = (1, 0)
VECTOR_COLUMNS = (128, 0)
ELSEWHERE = ((1, 1), (2, 1), (3, 1), (5, 1))
PE_PIECES = (1, 3, 5, 7)

FLOPS = 2 * SAMPLES * ORDERS * NODES * NODES * CHANNELS
BYTES = 2 * (2 * NODES * NODES + SAMPLES * NODES * NODES + 3 * SAMPLES * NODES * CHANNELS) + 4 * SAMPLES * NODES * CHANNELS


def tile_napl_conv_withsat_pb_kernel(tc, supports, cheb_2, spatial_attention, x, grad_out, out):
    nc = tc.nc

    supports_v = supports.rearrange("(i p) m -> i p m", p=P)
    cheb_2_v = cheb_2.rearrange("(i p) m -> i p m", p=P)
    attention_v = spatial_attention.rearrange("b (i p) m -> b i p m", p=P)
    grad_v = grad_out.rearrange("k b m f t -> k b m (f t)")
    grad_0_v = grad_v[0].rearrange("b (i p) c -> b i p c", p=P)
    out_v = out.rearrange("b (i p) f t -> b i p (f t)", p=P)
    diagonal_v = spatial_attention.rearrange("b n m -> b (n m)")[:, 0 : NODES * NODES : NODES + 1].rearrange("b (i p) -> b p i", p=P)

    with ExitStack() as stack:
        stack.enter_context(tc.manual_schedule())
        keep = stack.enter_context(tc.tile_pool(name="keep", bufs=1))
        stage = stack.enter_context(tc.tile_pool(name="stage", bufs=2))
        results = stack.enter_context(tc.tile_pool(name="results", bufs=10))
        flipped = stack.enter_context(tc.psum_pool(name="flipped", bufs=2))
        sums = stack.enter_context(tc.psum_pool(name="sums", bufs=4))

        pieces = [(b, o, g) for b in range(SAMPLES) for o in range(ORDERS) for g in range(PASSES)]
        pieces_a_sample = ORDERS * PASSES
        supports_raw, cheb_2_raw, attention_raw, grad_0_raw, grad_raw = {}, {}, {}, {}, {}

        def load_rows(view, name):
            raw = keep.tile([P, NODES], BF16, name=name)
            nc.sync.dma_start(out=raw[:], in_=view)
            return raw

        def load_matrices(i):
            supports_raw[i] = load_rows(supports_v[i], "supports_raw_%d" % i)
            attention_raw[(0, i)] = load_rows(attention_v[0, i], "attention_raw_%d_%d" % (0, i))
            cheb_2_raw[i] = load_rows(cheb_2_v[i], "cheb_2_raw_%d" % i)
            attention_raw[(1, i)] = load_rows(attention_v[1, i], "attention_raw_%d_%d" % (1, i))

        def load_grad_0(i, b):
            grad_0_raw[(i, b)] = keep.tile([P, CHANNELS], BF16, name="grad_0_raw_%d_%d" % (i, b))
            nc.sync.dma_start(out=grad_0_raw[(i, b)][:], in_=grad_0_v[b, i])

        def load_grad_piece(b, o, g):
            raw = keep.tile([P, PACK, CHANNELS], BF16, name="grad_raw_%d_%d_%d" % (b, o, g))
            rows = grad_v[o + 1, b].rearrange("(g u p e) c -> g p u (e c)", g=PASSES, u=2, e=2)
            nc.sync.dma_start(out=raw[:].rearrange("p (u e) c -> p u (e c)", u=2), in_=rows[g])
            grad_raw[(b, o, g)] = raw

        half_tiles = ROW_TILES // 2
        diagonal = {}

        def load_diagonal(b, h):
            diagonal[(b, h)] = keep.tile([P, half_tiles], BF16, name="diagonal_%d_%d" % (b, h))
            with nc.allow_non_contiguous_dma(reason="512 diagonal elements, one to a row of the attention"):
                nc.sync.dma_start(out=diagonal[(b, h)][:], in_=diagonal_v[b][:, h * half_tiles : (h + 1) * half_tiles])

        def pieces_of_step(s):
            return pieces[s * PIECES_A_STEP : (s + 1) * PIECES_A_STEP]

        def load_for_adds(s):
            if s == 1:
                load_diagonal(0, 0)
                load_grad_0(0, 0)
            if s == 3:
                load_diagonal(1, 0)
            if s == 4:
                load_diagonal(0, 1)
                load_diagonal(1, 1)
            if 1 <= s < ROW_TILES:
                load_grad_0(s, 0)
            if s >= 3:
                for i in (2 * (s - 3), 2 * (s - 3) + 1):
                    if i < ROW_TILES:
                        load_grad_0(i, 1)

        load_matrices(0)
        for s in range(ROW_TILES + 1):
            for piece in pieces_of_step(s):
                load_grad_piece(*piece)
            if s >= 1:
                load_for_adds(s - 1)
            if s + 1 < ROW_TILES:
                load_matrices(s + 1)

        identity = keep.tile([P, P], F32)
        make_identity(nc, identity[:])
        identity_bf16 = keep.tile([P, P], BF16)
        make_identity(nc, identity_bf16[:])
        grad_grouped, grad_codes, grad_scales = {}, {}, {}

        def regroup_grad_piece(piece):
            raw = grad_raw[piece]
            grouped = stage.tile([P, CHANNELS, PACK], BF16, name="grad_grouped", bufs=3, align_bytes=64)
            if pieces.index(piece) in PE_PIECES:
                half = CHANNELS // 2
                for h in range(2):
                    bank = sums.tile([P, half, PACK], BF16, name="unit_sums")
                    for q in range(2):
                        cols = slice(h * half + q * P, h * half + (q + 1) * P)
                        nc.tensor.matmul(
                            out=bank[:, q * P : (q + 1) * P, :].rearrange("p c t -> p (c t)"),
                            lhsT=identity_bf16[:],
                            rhs=raw[:, :, cols].rearrange("p t c -> p c t"),
                            start=True,
                            stop=True,
                        )
                    nc.scalar.copy(out=grouped[:, h * half : (h + 1) * half, :], in_=bank[:])
                grad_grouped[piece] = grouped
                return
            split = VECTOR_COLUMNS[piece[0]]
            if split:
                nc.vector.tensor_copy(
                    out=grouped[:, :split, :].rearrange("p (c i) t -> p c t i", i=4),
                    in_=raw[:, :, :split].rearrange("p t (c i) -> p c t i", i=4),
                )
            nc.scalar.copy(
                out=grouped[:, split:, :].rearrange("p (c i) t -> p c t i", i=4),
                in_=raw[:, :, split:].rearrange("p t (c i) -> p c t i", i=4),
            )
            grad_grouped[piece] = grouped

        def quantise_grad_piece(piece):
            codes = keep.tile([P, CHANNELS], U32, name="grad_codes_%d_%d_%d" % piece, align_bytes=64)
            scales = keep.tile([P, CHANNELS], U8, name="grad_scales_%d_%d_%d" % piece, align_bytes=64)
            nc.vector.quantize_mx(
                out=codes[:].bitcast(E5M2_X4),
                scales=scales[:],
                in_=grad_grouped[piece][:].rearrange("p c t -> p (c t)"),
            )
            grad_codes[piece] = codes
            grad_scales[piece] = scales

        weights_t, attention_t, products, product_codes, product_scales, unit_sums = {}, {}, {}, {}, {}, {}

        def flip(i):
            weights_t[i] = stage.tile([P, ORDERS, NODES], BF16, name="weights_t")

            def flip_weights(o):
                raw = (supports_raw[i], cheb_2_raw[i])[o]
                bank = flipped.tile([P, FLIPS, P], F32, name="weights_bank")
                for j in range(FLIPS):
                    nc.tensor.transpose(bank[:, j, :], raw[:].bitcast(F32)[:, j * P : (j + 1) * P], identity[:])
                nc.scalar.copy(
                    out=weights_t[i][:, o, :].bitcast(F32).rearrange("p (g n u) -> p g n u", g=PASSES, u=2),
                    in_=bank[:].rearrange("p (g u) n -> p g n u", u=2),
                )

            def flip_attention(b):
                bank = flipped.tile([P, PASSES, P, 2], F32, name="attention_bank")
                for j in range(FLIPS):
                    g, u = divmod(j, 2)
                    nc.tensor.transpose(bank[:, g, :, u], attention_raw[(b, i)][:].bitcast(F32)[:, j * P : (j + 1) * P], identity[:])
                attention_t[(b, i)] = bank

            if i == 0:
                flip_weights(0)
                flip_attention(0)
                flip_weights(1)
                flip_attention(1)
            else:
                flip_weights(0)
                flip_weights(1)
                flip_attention(0)
                flip_attention(1)

        def multiply(i):
            products[i] = stage.tile([P, SAMPLES, ORDERS, NODES], BF16, name="products", align_bytes=64)
            for b in range(SAMPLES):
                attention_bf16 = attention_t[(b, i)][:].rearrange("p g n u -> p (g n u)").bitcast(BF16)
                if i == 0 and b == 0:
                    for o in range(ORDERS):
                        nc.vector.tensor_tensor(out=products[i][:, b, o], in0=weights_t[i][:, o], in1=attention_bf16, op=MULT)
                    continue
                nc.vector.tensor_tensor(
                    out=products[i][:, b],
                    in0=weights_t[i][:],
                    in1=attention_bf16.unsqueeze(1).to_broadcast([P, ORDERS, NODES]),
                    op=MULT,
                )

        def quantise(i):
            product_codes[i] = stage.tile([P, len(pieces) * P], U32, name="product_codes", bufs=5, align_bytes=64)
            product_scales[i] = stage.tile([P, len(pieces) * P], U8, name="product_scales", bufs=5, align_bytes=64)
            nc.vector.quantize_mx(
                out=product_codes[i][:].bitcast(E4M3_X4),
                scales=product_scales[i][:],
                in_=products[i][:].rearrange("p b o k -> p (b o k)"),
            )

        def quantise_sample(i, b):
            if b == 0:
                product_codes[i] = stage.tile([P, len(pieces) * P], U32, name="product_codes", bufs=5, align_bytes=64)
                product_scales[i] = stage.tile([P, len(pieces) * P], U8, name="product_scales", bufs=5, align_bytes=64)
            cols = slice(b * pieces_a_sample * P, (b + 1) * pieces_a_sample * P)
            nc.vector.quantize_mx(
                out=product_codes[i][:, cols].bitcast(E4M3_X4),
                scales=product_scales[i][:, cols],
                in_=products[i][:, b].rearrange("p o k -> p (o k)"),
            )

        def contract(i, b):
            unit_sums[(i, b)] = sums.tile([P, CHANNELS], F32, name="unit_sums")
            for index in range(pieces_a_sample):
                piece = pieces[b * pieces_a_sample + index]
                n_cols = slice((b * pieces_a_sample + index) * P, (b * pieces_a_sample + index + 1) * P)
                nc.tensor.matmul_mx(
                    out=unit_sums[(i, b)][:],
                    lhsT=product_codes[i][:, n_cols].bitcast(E4M3_X4),
                    lhsT_scale=product_scales[i][:, n_cols],
                    rhs=grad_codes[piece][:].bitcast(E5M2_X4),
                    rhs_scale=grad_scales[piece][:],
                    start=(index == 0),
                    stop=(index == pieces_a_sample - 1),
                )

        diagonal_f32 = {}

        def finish_elsewhere(i, b):
            h = i // half_tiles
            if (b, h) not in diagonal_f32:
                diagonal_f32[(b, h)] = keep.tile([P, half_tiles], F32, name="diagonal_f32_%d_%d" % (b, h))
                nc.gpsimd.tensor_copy(out=diagonal_f32[(b, h)][:], in_=diagonal[(b, h)][:])
            result = results.tile([P, CHANNELS], F32, name="result")
            first_term = stage.tile([P, CHANNELS], F32, name="first_term")
            nc.scalar.activation(out=first_term[:], in_=grad_0_raw[(i, b)][:], func=COPY, scale=diagonal_f32[(b, h)][:, i % half_tiles : i % half_tiles + 1])
            sums_copy = stage.tile([P, CHANNELS], F32, name="sums_copy")
            nc.scalar.copy(out=sums_copy[:], in_=unit_sums[(i, b)][:])
            nc.gpsimd.tensor_tensor(out=result[:], in0=first_term[:], in1=sums_copy[:], op=ADD)
            nc.sync.dma_start(out=out_v[b, i], in_=result[:])

        def finish(units):
            for i, b in units:
                result = results.tile([P, CHANNELS], F32, name="result")
                nc.vector.scalar_tensor_tensor(
                    out=result[:],
                    in0=grad_0_raw[(i, b)][:],
                    scalar=diagonal[(b, i // half_tiles)][:, i % half_tiles : i % half_tiles + 1],
                    in1=unit_sums[(i, b)][:],
                    op0=MULT,
                    op1=ADD,
                )
                nc.sync.dma_start(out=out_v[b, i], in_=result[:])

        waiting = [[] for b in range(SAMPLES)]
        contracted = []
        flip(0)
        for s in range(ROW_TILES + 1):
            last_tile = s == ROW_TILES - 1
            if s < ROW_TILES:
                multiply(s)
            for piece in pieces_of_step(s):
                regroup_grad_piece(piece)
            if s + 1 < ROW_TILES:
                flip(s + 1)
            if last_tile:
                for b in range(SAMPLES):
                    quantise_sample(s, b)
            held_back = 1 if (s < ROW_TILES and not last_tile and len(contracted) > 1) else 0
            finish(contracted[: len(contracted) - held_back])
            if s < ROW_TILES and not last_tile:
                quantise(s)
            finish(contracted[len(contracted) - held_back :])
            contracted = []
            for piece in pieces_of_step(s):
                quantise_grad_piece(piece)
            for b in B_ORDER:
                if s < ROW_TILES:
                    waiting[b].append(s)
                if (s + 1) * PIECES_A_STEP >= (b + 1) * pieces_a_sample:
                    quota = CATCH_UP if b == 0 else B1_QUOTA.get(s, CATCH_UP)
                    for i in waiting[b][:quota]:
                        contract(i, b)
                        if (i, b) in ELSEWHERE:
                            finish_elsewhere(i, b)
                        else:
                            contracted.append((i, b))
                    waiting[b] = waiting[b][quota:]
